import numpy as np
import ml_dtypes


def mxq(x, axis, fmt="e4m3"):
    dtype, down = {"e4m3": (ml_dtypes.float8_e4m3fn, 7), "e5m2": (ml_dtypes.float8_e5m2, 14)}[fmt]
    v = np.moveaxis(np.asarray(x, np.float32).astype(ml_dtypes.bfloat16).astype(np.float64), axis, -1)
    blocks = v.reshape(v.shape[:-1] + (-1, 32))
    amax = np.abs(blocks).max(-1, keepdims=True)
    byte = np.maximum(np.where(amax > 0, np.frexp(amax)[1] - 1 + 127, 0) - down, 1)
    scale = np.exp2(byte - 127.0)
    codes = (blocks / scale).astype(np.float32).astype(dtype).astype(np.float64)
    return np.moveaxis((codes * scale).reshape(v.shape), -1, axis)


WIDE = False


def mx_kscale(k):
    if not WIDE:
        return np.ones(k)
    levels = np.array([10, -10, 5, -5, 0])
    a = np.random.permutation(np.resize(levels, k // 512 * 4)).reshape(k // 512, 4)
    idx = np.arange(k)
    return np.exp2(a[idx // 512, idx % 128 // 32])


BF16 = ml_dtypes.bfloat16


def bf(x):
    return np.asarray(x, np.float32).astype(BF16)


def f64(x):
    return np.asarray(x).astype(np.float64)


N, C, H, W, BINS = 8, 2, 32, 32, 512
SIGMA = 0.05


def setup_inputs():
    u = np.random.random_sample((N, H, W))[:, None]
    v = np.random.random_sample((N, C, H, W))
    img = 0.6 * u + 0.4 * v
    e = np.log2(mx_kscale(H * W)).reshape(H, W)
    m = np.abs(e).max()
    if m > 0:
        dn = np.stack([m - e, m + e])
        img = -np.sqrt((0.1 * img) ** 2 + 2.0 * np.log(2.0) * SIGMA ** 2 * dn)
    return {"image": bf(img)}


def reference(image):
    image = f64(image)
    n, c, h, w = image.shape
    bins = np.linspace(0.0, 1.0, BINS)
    ch_a = image[:, 0].reshape(n, h * w)
    ch_b = image[:, 1].reshape(n, h * w)
    inv_sigma = 1.0 / SIGMA
    ka = np.exp(-0.5 * ((ch_a[:, :, None] - bins) * inv_sigma) ** 2)
    kb = np.exp(-0.5 * ((ch_b[:, :, None] - bins) * inv_sigma) ** 2)
    hist = mxq(ka, 1, "e4m3").transpose(0, 2, 1) @ mxq(kb, 1, "e4m3")
    return hist[:, None, :, :]

@@ -1,0 +1,123 @@
+import concourse.mybir as mybir
+
+F32 = mybir.dt.float32
+BF16 = mybir.dt.bfloat16
+I32 = mybir.dt.int32
+U32 = mybir.dt.uint32
+U8 = mybir.dt.uint8
+FP8X4 = mybir.dt.float8_e4m3fn_x4
+ACT = mybir.ActivationFunctionType
+ALU = mybir.AluOpType
+
+P = 128
+PACK = 4
+N_IMG = 8
+BINS = 512
+PASSES = 2
+KAPPA = 200.0
+FLOPS = 2 * N_IMG * BINS * BINS * 1024
+
+
+def tile_colourhistogram_t_kernel(tc, image, out):
+    nc = tc.nc
+    pix = image.rearrange("n c (g hp) (wp j) -> (hp wp) (n c g) j", g=PASSES, hp=16, wp=8, j=PACK)
+    with tc.tile_pool(name="const", bufs=1) as const, tc.tile_pool(name="ework", bufs=3) as ework, tc.tile_pool(
+        name="gwork", bufs=3
+    ) as gwork, tc.tile_pool(name="quant", bufs=8) as quant, tc.tile_pool(name="store", bufs=6) as store, tc.psum_pool(
+        name="acc", bufs=8
+    ) as accp:
+        first = 4
+        a0 = const.tile([P, first, PACK], BF16)
+        a1 = const.tile([P, 32 - first, PACK], BF16)
+        nc.sync.dma_start(out=a0[:], in_=pix[:, 0:first, :])
+        nc.sync.dma_start(out=a1[:], in_=pix[:, first:32, :])
+
+        idx = const.tile([P, BINS], I32)
+        nc.gpsimd.iota(idx[:], pattern=[[1, BINS]], base=0, channel_multiplier=0)
+        r = const.tile([P, BINS], F32)
+        nc.vector.tensor_scalar(out=r[:], in0=idx[:], scalar1=-255.5, scalar2=1.0 / 511.0, op0=ALU.add, op1=ALU.mult)
+        r2 = const.tile([P, BINS], F32)
+        nc.scalar.activation(out=r2[:], in_=r[:], func=ACT.Square)
+        gw = const.tile([P, BINS], F32)
+        nc.scalar.activation(out=gw[:], in_=r2[:], func=ACT.Exp, scale=-KAPPA)
+
+        def affine(a, cols, label):
+            v = const.tile([P, cols * PACK], F32, name="v" + label)
+            sc = const.tile([P, cols * PACK], F32, name="sc" + label)
+            bi = const.tile([P, cols * PACK], F32, name="bi" + label)
+            flat = a[:].rearrange("p m j -> p (m j)")
+            nc.vector.tensor_scalar(out=v[:], in0=flat, scalar1=-0.5, scalar2=None, op0=ALU.add)
+            nc.vector.tensor_scalar(out=sc[:], in0=flat, scalar1=-0.5, scalar2=2.0 * KAPPA, op0=ALU.add, op1=ALU.mult)
+            nc.vector.scalar_tensor_tensor(out=bi[:], in0=v[:], scalar=-KAPPA, in1=v[:], op0=ALU.mult, op1=ALU.mult)
+            return sc, bi
+
+        sc0, bi0 = affine(a0, first, "0")
+        sc1, bi1 = affine(a1, 32 - first, "1")
+
+        def column(m, j):
+            if m < first:
+                q = m * PACK + j
+                return sc0[:, q : q + 1], bi0[:, q : q + 1]
+            q = (m - first) * PACK + j
+            return sc1[:, q : q + 1], bi1[:, q : q + 1]
+
+        units = [(n, g, c) for n in range(N_IMG) for g in range(PASSES) for c in range(2)]
+        grouped_of = {}
+        codes_of = {}
+        acc_of = {}
+
+        def make(u):
+            n, g, c = units[u]
+            m = (n * 2 + c) * PASSES + g
+            e1 = ework.tile([P, PACK, BINS], F32)
+            for j in range(PACK):
+                sc, bi = column(m, j)
+                nc.scalar.activation(out=e1[:, j, :], in_=r[:], func=ACT.Exp, bias=bi, scale=sc)
+            grouped = gwork.tile([P, BINS, PACK], BF16, align_bytes=64)
+            nc.vector.tensor_tensor(
+                out=grouped[:],
+                in0=e1[:].rearrange("p j w -> p w j"),
+                in1=gw[:].unsqueeze(2).to_broadcast([P, BINS, PACK]),
+                op=ALU.mult,
+            )
+            grouped_of[u] = grouped
+
+        def finish(u):
+            n, g, c = units[u]
+            codes = quant.tile([P, BINS], U32, align_bytes=64)
+            scales = quant.tile([P, BINS], U8, align_bytes=64)
+            nc.vector.quantize_mx(
+                out=codes[:].bitcast(FP8X4),
+                scales=scales[:],
+                in_=grouped_of[u][:].rearrange("p w j -> p (w j)"),
+            )
+            codes_of[(n, g, c)] = (codes, scales)
+            if c == 0:
+                return
+            ka, ka_s = codes_of[(n, g, 0)]
+            kb, kb_s = codes_of[(n, g, 1)]
+            for t in range(4):
+                if g == 0:
+                    acc = accp.tile([P, BINS], F32)
+                    acc_of[(n, t)] = acc
+                cols = slice(t * P, (t + 1) * P)
+                nc.tensor.matmul_mx(
+                    out=acc_of[(n, t)][:],
+                    lhsT=ka[:, cols].bitcast(FP8X4),
+                    lhsT_scale=ka_s[:, cols],
+                    rhs=kb[:].bitcast(FP8X4),
+                    rhs_scale=kb_s[:],
+                    start=(g == 0),
+                    stop=(g == PASSES - 1),
+                )
+            if g == PASSES - 1:
+                for t in range(4):
+                    res = store.tile([P, BINS], F32)
+                    nc.scalar.copy(out=res[:], in_=acc_of[(n, t)][:])
+                    nc.sync.dma_start(out=out[n, 0, t * P : (t + 1) * P, :], in_=res[:])
+
+        for u in range(len(units) + 1):
+            if u < len(units):
+                make(u)
+            if u >= 1:
+                finish(u - 1)

@@ -14,6 +14,7 @@ PACK = 4
 N_IMG = 8
 BINS = 512
 PASSES = 2
+RUN = 4
 KAPPA = 200.0
 FLOPS = 2 * N_IMG * BINS * BINS * 1024
 
@@ -75,9 +76,9 @@ def tile_colourhistogram_t_kernel(tc, image, out):
                 nc.scalar.activation(out=e1[:, j, :], in_=r[:], func=ACT.Exp, bias=bi, scale=sc)
             grouped = gwork.tile([P, BINS, PACK], BF16, align_bytes=64)
             nc.vector.tensor_tensor(
-                out=grouped[:],
-                in0=e1[:].rearrange("p j w -> p w j"),
-                in1=gw[:].unsqueeze(2).to_broadcast([P, BINS, PACK]),
+                out=grouped[:].rearrange("p (c i) j -> p c j i", i=RUN),
+                in0=e1[:].rearrange("p j (c i) -> p c j i", i=RUN),
+                in1=gw[:].rearrange("p (c i) -> p c i", i=RUN).unsqueeze(2).to_broadcast([P, BINS // RUN, PACK, RUN]),
                 op=ALU.mult,
             )
             grouped_of[u] = grouped

@@ -1,4 +1,5 @@
 import concourse.mybir as mybir
+from concourse.masks import make_identity
 
 F32 = mybir.dt.float32
 BF16 = mybir.dt.bfloat16
@@ -8,6 +9,7 @@ U8 = mybir.dt.uint8
 FP8X4 = mybir.dt.float8_e4m3fn_x4
 ACT = mybir.ActivationFunctionType
 ALU = mybir.AluOpType
+AX = mybir.AxisListType
 
 P = 128
 PACK = 4
@@ -17,16 +19,24 @@ PASSES = 2
 RUN = 4
 KAPPA = 200.0
 FLOPS = 2 * N_IMG * BINS * BINS * 1024
+PE_IMAGES = (2, 3, 4, 5, 6, 7)
+SCALAR_DRAINS = (4, 3, 2, 2, 2, 3, 4)
+LAST_SCALAR_DRAINS = 2
+ARG_AHEAD = 4
+FIRST_ARG_STEP = 3
+STATION_STEP = 1
+ORDER = ((0, 0), (0, 1), (1, 1), (1, 0))
 
 
 def tile_colourhistogram_t_kernel(tc, image, out):
     nc = tc.nc
     pix = image.rearrange("n c (g hp) (wp j) -> (hp wp) (n c g) j", g=PASSES, hp=16, wp=8, j=PACK)
-    with tc.tile_pool(name="const", bufs=1) as const, tc.tile_pool(name="ework", bufs=3) as ework, tc.tile_pool(
-        name="gwork", bufs=3
+    n_pe = len(PE_IMAGES)
+    with tc.tile_pool(name="const", bufs=1) as const, tc.tile_pool(name="ework", bufs=4) as ework, tc.tile_pool(
+        name="gwork", bufs=4
     ) as gwork, tc.tile_pool(name="quant", bufs=8) as quant, tc.tile_pool(name="store", bufs=6) as store, tc.psum_pool(
-        name="acc", bufs=8
-    ) as accp:
+        name="accp", bufs=4
+    ) as accp, tc.psum_pool(name="argp", bufs=4) as argp, tc.manual_schedule():
         first = 4
         a0 = const.tile([P, first, PACK], BF16)
         a1 = const.tile([P, 32 - first, PACK], BF16)
@@ -35,6 +45,11 @@ def tile_colourhistogram_t_kernel(tc, image, out):
 
         idx = const.tile([P, BINS], I32)
         nc.gpsimd.iota(idx[:], pattern=[[1, BINS]], base=0, channel_multiplier=0)
+        ident = const.tile([P, P], F32)
+        make_identity(nc, ident[:])
+        spread = const.tile([P, n_pe, P], F32)
+        nc.gpsimd.memset(spread[:], 0.0)
+
         r = const.tile([P, BINS], F32)
         nc.vector.tensor_scalar(out=r[:], in0=idx[:], scalar1=-255.5, scalar2=1.0 / 511.0, op0=ALU.add, op1=ALU.mult)
         r2 = const.tile([P, BINS], F32)
@@ -53,51 +68,135 @@ def tile_colourhistogram_t_kernel(tc, image, out):
             return sc, bi
 
         sc0, bi0 = affine(a0, first, "0")
-        sc1, bi1 = affine(a1, 32 - first, "1")
+
+        head = ident[:, 0 : 3 * PACK]
+        term = const.tile([P, 3], F32)
+        nc.vector.tensor_reduce(out=term[:], in_=head.rearrange("k (j t) -> k t j", t=3), axis=AX.X, op=ALU.add)
+        place = const.tile([P, PACK], F32)
+        nc.vector.tensor_reduce(out=place[:], in_=head.rearrange("k (j t) -> k j t", t=3), axis=AX.X, op=ALU.add)
+        quad = const.tile([P, 1], F32)
+        nc.vector.tensor_scalar(out=quad[:], in0=term[:, 2:3], scalar1=-KAPPA, scalar2=None, op0=ALU.mult)
+        lin = const.tile([P, BINS], F32)
+        nc.vector.tensor_scalar(
+            out=lin[:], in0=r[:], scalar1=term[:, 0:1], scalar2=term[:, 1:2], op0=ALU.mult, op1=ALU.add
+        )
+        rows = const.tile([P, BINS], F32)
+        nc.vector.scalar_tensor_tensor(
+            out=rows[:], in0=r2[:], scalar=quad[:, 0:1], in1=lin[:], op0=ALU.mult, op1=ALU.add
+        )
+        moving = const.tile([P, BINS, PACK], F32)
+        nc.vector.tensor_tensor(
+            out=moving[:],
+            in0=rows[:].unsqueeze(2).to_broadcast([P, BINS, PACK]),
+            in1=place[:].unsqueeze(1).to_broadcast([P, BINS, PACK]),
+            op=ALU.mult,
+        )
+        moving_flat = moving[:].rearrange("k w j -> k (w j)")
+        station = const.tile([P, n_pe, P], F32)
+        later = {}
+
+        def spread_and_turn():
+            sc1, bi1 = later["affine"]
+            lo = 4 * PE_IMAGES[0] + 1 - first
+            hi = 4 * PE_IMAGES[-1] + 1 - first + 1
+            spread_v = spread[:, :, 0 : 3 * PACK].rearrange("p i (j t) -> p t i j", t=3)
+            nc.vector.tensor_copy(out=spread_v[:, 0], in_=sc1[:].rearrange("p (m j) -> p m j", j=PACK)[:, lo:hi:4, :])
+            nc.vector.tensor_copy(out=spread_v[:, 1], in_=bi1[:].rearrange("p (m j) -> p m j", j=PACK)[:, lo:hi:4, :])
+            nc.vector.memset(spread_v[:, 2], 1.0)
+            for b in range(0, n_pe, 4):
+                e = min(b + 4, n_pe)
+                turned = argp.tile([P, BINS], F32, tag="arg")
+                later[b] = turned
+                for i in range(b, e):
+                    nc.tensor.transpose(turned[:, (i - b) * P : (i - b + 1) * P], spread[:, i, :], ident[:])
+
+        def stationary_operands():
+            for b in range(0, n_pe, 4):
+                e = min(b + 4, n_pe)
+                nc.vector.tensor_copy(
+                    out=station[:, b:e, :].rearrange("k i p -> k (i p)"), in_=later[b][:, 0 : (e - b) * P]
+                )
 
         def column(m, j):
             if m < first:
                 q = m * PACK + j
                 return sc0[:, q : q + 1], bi0[:, q : q + 1]
+            sc1, bi1 = later["affine"]
             q = (m - first) * PACK + j
             return sc1[:, q : q + 1], bi1[:, q : q + 1]
 
-        units = [(n, g, c) for n in range(N_IMG) for g in range(PASSES) for c in range(2)]
+        units = [(n, g, c) for n in range(N_IMG) for (g, c) in ORDER]
         grouped_of = {}
         codes_of = {}
         acc_of = {}
+        arg_of = {}
+        e1_of = {}
 
-        def make(u):
+        def from_tensor_engine(u):
             n, g, c = units[u]
+            return n in PE_IMAGES and (g, c) == ORDER[3]
+
+        def exponent_matmuls(n, chunks):
+            for s in chunks:
+                arg = argp.tile([P, BINS], F32, tag="arg")
+                arg_of[(n, s)] = arg
+                nc.tensor.matmul(
+                    out=arg[:],
+                    lhsT=station[:, PE_IMAGES.index(n), :],
+                    rhs=moving_flat[:, s * BINS : (s + 1) * BINS],
+                    start=True,
+                    stop=True,
+                )
+
+        def exponentials(u):
+            n, g, c = units[u]
+            if from_tensor_engine(u):
+                grouped = gwork.tile([P, BINS, PACK], BF16, align_bytes=64)
+                grouped_of[u] = grouped
+                flat = grouped[:].rearrange("p w j -> p (w j)")
+                for s in range(4):
+                    nc.scalar.activation(out=flat[:, s * BINS : (s + 1) * BINS], in_=arg_of[(n, s)][:], func=ACT.Exp)
+                return
             m = (n * 2 + c) * PASSES + g
             e1 = ework.tile([P, PACK, BINS], F32)
+            e1_of[u] = e1
             for j in range(PACK):
                 sc, bi = column(m, j)
                 nc.scalar.activation(out=e1[:, j, :], in_=r[:], func=ACT.Exp, bias=bi, scale=sc)
+
+        def product(u):
+            if from_tensor_engine(u):
+                return
+            e1 = e1_of[u]
             grouped = gwork.tile([P, BINS, PACK], BF16, align_bytes=64)
+            grouped_of[u] = grouped
             nc.vector.tensor_tensor(
                 out=grouped[:].rearrange("p (c i) j -> p c j i", i=RUN),
                 in0=e1[:].rearrange("p j (c i) -> p c j i", i=RUN),
                 in1=gw[:].rearrange("p (c i) -> p c i", i=RUN).unsqueeze(2).to_broadcast([P, BINS // RUN, PACK, RUN]),
                 op=ALU.mult,
             )
-            grouped_of[u] = grouped
 
-        def finish(u):
-            n, g, c = units[u]
+        def quantise(u, pieces):
             codes = quant.tile([P, BINS], U32, align_bytes=64)
             scales = quant.tile([P, BINS], U8, align_bytes=64)
-            nc.vector.quantize_mx(
-                out=codes[:].bitcast(FP8X4),
-                scales=scales[:],
-                in_=grouped_of[u][:].rearrange("p w j -> p (w j)"),
-            )
-            codes_of[(n, g, c)] = (codes, scales)
-            if c == 0:
-                return
+            codes_of[units[u]] = (codes, scales)
+            flat = grouped_of[u][:].rearrange("p w j -> p (w j)")
+            width = BINS // pieces
+            for s in range(pieces):
+                cols = slice(s * width, (s + 1) * width)
+                nc.vector.quantize_mx(
+                    out=codes[:, cols].bitcast(FP8X4),
+                    scales=scales[:, cols],
+                    in_=flat[:, s * width * PACK : (s + 1) * width * PACK],
+                )
+                if pieces > 1:
+                    passes(units[u][0], units[u][1], [s])
+
+        def passes(n, g, blocks):
             ka, ka_s = codes_of[(n, g, 0)]
             kb, kb_s = codes_of[(n, g, 1)]
-            for t in range(4):
+            for t in blocks:
                 if g == 0:
                     acc = accp.tile([P, BINS], F32)
                     acc_of[(n, t)] = acc
@@ -111,14 +210,58 @@ def tile_colourhistogram_t_kernel(tc, image, out):
                     start=(g == 0),
                     stop=(g == PASSES - 1),
                 )
-            if g == PASSES - 1:
-                for t in range(4):
-                    res = store.tile([P, BINS], F32)
-                    nc.scalar.copy(out=res[:], in_=acc_of[(n, t)][:])
-                    nc.sync.dma_start(out=out[n, 0, t * P : (t + 1) * P, :], in_=res[:])
 
-        for u in range(len(units) + 1):
-            if u < len(units):
-                make(u)
-            if u >= 1:
-                finish(u - 1)
+        def drains(n, on_scalar):
+            for t in range(4):
+                res = store.tile([P, BINS], F32)
+                if t < on_scalar:
+                    nc.scalar.copy(out=res[:], in_=acc_of[(n, t)][:])
+                else:
+                    nc.vector.tensor_copy(out=res[:], in_=acc_of[(n, t)][:])
+                nc.sync.dma_start(out=out[n, 0, t * P : (t + 1) * P, :], in_=res[:])
+
+        last = N_IMG - 1
+        for u in range(len(units)):
+            n, g, c = units[u]
+            pos = u % 4
+            if u == FIRST_ARG_STEP:
+                exponent_matmuls(PE_IMAGES[0], range(4))
+            exponentials(u)
+            if pos == 0:
+                product(u)
+                if n >= 1 and units[u - 1] not in codes_of:
+                    quantise(u - 1, 1)
+                    passes(n - 1, 1, range(4))
+            elif pos == 1:
+                product(u)
+                quantise(u - 1, 1)
+            elif pos == 2 and n == last:
+                quantise(u - 1, 1)
+                drains(n - 1, SCALAR_DRAINS[n - 1])
+                passes(n, 0, range(4))
+                product(u)
+            elif pos == 2:
+                product(u)
+                quantise(u - 1, 1)
+            else:
+                if from_tensor_engine(u) and n < last:
+                    exponent_matmuls(n + 1, range(ARG_AHEAD))
+                product(u)
+                quantise(u - 1, 1)
+                if n < last:
+                    if n >= 1:
+                        drains(n - 1, SCALAR_DRAINS[n - 1])
+                    passes(n, 0, range(4))
+                if from_tensor_engine(u):
+                    if n == last:
+                        quantise(u, 4)
+                    else:
+                        quantise(u, 1)
+                        passes(n, 1, range(4))
+                        exponent_matmuls(n + 1, range(ARG_AHEAD, 4))
+            if u == 0:
+                later["affine"] = affine(a1, 32 - first, "1")
+                spread_and_turn()
+            if u == STATION_STEP:
+                stationary_operands()
+        drains(last, LAST_SCALAR_DRAINS)

@@ -20,23 +20,24 @@ RUN = 4
 KAPPA = 200.0
 FLOPS = 2 * N_IMG * BINS * BINS * 1024
 PE_IMAGES = (2, 3, 4, 5, 6, 7)
-SCALAR_DRAINS = (4, 3, 2, 2, 2, 3, 4)
-LAST_SCALAR_DRAINS = 2
-ARG_AHEAD = 4
-FIRST_ARG_STEP = 3
-STATION_STEP = 1
-ORDER = ((0, 0), (0, 1), (1, 1), (1, 0))
+SCALAR_DRAINS = (4, 3, 0, 0, 0, 0, 4)
+LAST_SCALAR_DRAINS = 3
+GP_PIECES = 2
+A, B, C, D = (0, 0), (0, 1), (1, 1), (1, 0)
 
 
 def tile_colourhistogram_t_kernel(tc, image, out):
     nc = tc.nc
     pix = image.rearrange("n c (g hp) (wp j) -> (hp wp) (n c g) j", g=PASSES, hp=16, wp=8, j=PACK)
     n_pe = len(PE_IMAGES)
-    with tc.tile_pool(name="const", bufs=1) as const, tc.tile_pool(name="ework", bufs=4) as ework, tc.tile_pool(
-        name="gwork", bufs=4
-    ) as gwork, tc.tile_pool(name="quant", bufs=8) as quant, tc.tile_pool(name="store", bufs=6) as store, tc.psum_pool(
-        name="accp", bufs=4
-    ) as accp, tc.psum_pool(name="argp", bufs=4) as argp, tc.manual_schedule():
+    last = N_IMG - 1
+    with tc.tile_pool(name="const", bufs=1) as const, tc.tile_pool(name="ework", bufs=6) as ework, tc.tile_pool(
+        name="gwork", bufs=6
+    ) as gwork, tc.tile_pool(name="pwork", bufs=1) as pwork, tc.tile_pool(name="quant", bufs=8) as quant, tc.tile_pool(
+        name="store", bufs=6
+    ) as store, tc.psum_pool(name="accp", bufs=4) as accp, tc.psum_pool(name="argp", bufs=3) as argp, tc.psum_pool(
+        name="gpsum", bufs=1
+    ) as gpsum, tc.manual_schedule():
         first = 4
         a0 = const.tile([P, first, PACK], BF16)
         a1 = const.tile([P, 32 - first, PACK], BF16)
@@ -56,6 +57,8 @@ def tile_colourhistogram_t_kernel(tc, image, out):
         nc.scalar.activation(out=r2[:], in_=r[:], func=ACT.Square)
         gw = const.tile([P, BINS], F32)
         nc.scalar.activation(out=gw[:], in_=r2[:], func=ACT.Exp, scale=-KAPPA)
+        gw_psum = gpsum.tile([P, BINS], F32)
+        nc.tensor.matmul(out=gw_psum[:], lhsT=ident[:], rhs=gw[:], start=True, stop=True)
 
         def affine(a, cols, label):
             v = const.tile([P, cols * PACK], F32, name="v" + label)
@@ -93,10 +96,10 @@ def tile_colourhistogram_t_kernel(tc, image, out):
         )
         moving_flat = moving[:].rearrange("k w j -> k (w j)")
         station = const.tile([P, n_pe, P], F32)
-        later = {}
+        sc1, bi1 = affine(a1, 32 - first, "1")
+        turned_of = {}
 
         def spread_and_turn():
-            sc1, bi1 = later["affine"]
             lo = 4 * PE_IMAGES[0] + 1 - first
             hi = 4 * PE_IMAGES[-1] + 1 - first + 1
             spread_v = spread[:, :, 0 : 3 * PACK].rearrange("p i (j t) -> p t i j", t=3)
@@ -106,7 +109,7 @@ def tile_colourhistogram_t_kernel(tc, image, out):
             for b in range(0, n_pe, 4):
                 e = min(b + 4, n_pe)
                 turned = argp.tile([P, BINS], F32, tag="arg")
-                later[b] = turned
+                turned_of[b] = turned
                 for i in range(b, e):
                     nc.tensor.transpose(turned[:, (i - b) * P : (i - b + 1) * P], spread[:, i, :], ident[:])
 
@@ -114,74 +117,80 @@ def tile_colourhistogram_t_kernel(tc, image, out):
             for b in range(0, n_pe, 4):
                 e = min(b + 4, n_pe)
                 nc.vector.tensor_copy(
-                    out=station[:, b:e, :].rearrange("k i p -> k (i p)"), in_=later[b][:, 0 : (e - b) * P]
+                    out=station[:, b:e, :].rearrange("k i p -> k (i p)"), in_=turned_of[b][:, 0 : (e - b) * P]
                 )
 
         def column(m, j):
             if m < first:
                 q = m * PACK + j
                 return sc0[:, q : q + 1], bi0[:, q : q + 1]
-            sc1, bi1 = later["affine"]
             q = (m - first) * PACK + j
             return sc1[:, q : q + 1], bi1[:, q : q + 1]
 
-        units = [(n, g, c) for n in range(N_IMG) for (g, c) in ORDER]
         grouped_of = {}
         codes_of = {}
         acc_of = {}
         arg_of = {}
         e1_of = {}
 
-        def from_tensor_engine(u):
-            n, g, c = units[u]
-            return n in PE_IMAGES and (g, c) == ORDER[3]
+        def exponent_matmul(n, s):
+            arg = argp.tile([P, BINS], F32, tag="arg")
+            arg_of[(n, s)] = arg
+            nc.tensor.matmul(
+                out=arg[:],
+                lhsT=station[:, PE_IMAGES.index(n), :],
+                rhs=moving_flat[:, s * BINS : (s + 1) * BINS],
+                start=True,
+                stop=True,
+            )
 
-        def exponent_matmuls(n, chunks):
-            for s in chunks:
-                arg = argp.tile([P, BINS], F32, tag="arg")
-                arg_of[(n, s)] = arg
-                nc.tensor.matmul(
-                    out=arg[:],
-                    lhsT=station[:, PE_IMAGES.index(n), :],
-                    rhs=moving_flat[:, s * BINS : (s + 1) * BINS],
-                    start=True,
-                    stop=True,
-                )
-
-        def exponentials(u):
-            n, g, c = units[u]
-            if from_tensor_engine(u):
+        def exponential_of_bank(n, s):
+            if s == 0:
                 grouped = gwork.tile([P, BINS, PACK], BF16, align_bytes=64)
-                grouped_of[u] = grouped
-                flat = grouped[:].rearrange("p w j -> p (w j)")
-                for s in range(4):
-                    nc.scalar.activation(out=flat[:, s * BINS : (s + 1) * BINS], in_=arg_of[(n, s)][:], func=ACT.Exp)
-                return
+                grouped_of[(n, D)] = grouped
+            flat = grouped_of[(n, D)][:].rearrange("p w j -> p (w j)")
+            nc.scalar.activation(out=flat[:, s * BINS : (s + 1) * BINS], in_=arg_of[(n, s)][:], func=ACT.Exp)
+
+        def exponentials(n, unit):
+            g, c = unit
             m = (n * 2 + c) * PASSES + g
             e1 = ework.tile([P, PACK, BINS], F32)
-            e1_of[u] = e1
+            e1_of[(n, unit)] = e1
             for j in range(PACK):
                 sc, bi = column(m, j)
                 nc.scalar.activation(out=e1[:, j, :], in_=r[:], func=ACT.Exp, bias=bi, scale=sc)
 
-        def product(u):
-            if from_tensor_engine(u):
-                return
-            e1 = e1_of[u]
+        def product(n, unit):
             grouped = gwork.tile([P, BINS, PACK], BF16, align_bytes=64)
-            grouped_of[u] = grouped
+            grouped_of[(n, unit)] = grouped
             nc.vector.tensor_tensor(
                 out=grouped[:].rearrange("p (c i) j -> p c j i", i=RUN),
-                in0=e1[:].rearrange("p j (c i) -> p c j i", i=RUN),
-                in1=gw[:].rearrange("p (c i) -> p c i", i=RUN).unsqueeze(2).to_broadcast([P, BINS // RUN, PACK, RUN]),
+                in0=e1_of[(n, unit)][:].rearrange("p j (c i) -> p c j i", i=RUN),
+                in1=gw_psum[:]
+                .rearrange("p (c i) -> p c i", i=RUN)
+                .unsqueeze(2)
+                .to_broadcast([P, BINS // RUN, PACK, RUN]),
                 op=ALU.mult,
             )
 
-        def quantise(u, pieces):
+        def product_on_gpsimd(n, unit):
+            pgrouped = pwork.tile([P, BINS, PACK], BF16, align_bytes=64)
+            grouped_of[(n, unit)] = pgrouped
+            width = BINS // GP_PIECES
+            for h in range(GP_PIECES):
+                cols = slice(h * width, (h + 1) * width)
+                nc.gpsimd.tensor_tensor(
+                    out=pgrouped[:, cols, :],
+                    in0=e1_of[(n, unit)][:, :, cols].rearrange("p j w -> p w j"),
+                    in1=gw[:, cols].unsqueeze(2).to_broadcast([P, width, PACK]),
+                    op=ALU.mult,
+                )
+
+        def quantise(n, unit, pieces):
             codes = quant.tile([P, BINS], U32, align_bytes=64)
             scales = quant.tile([P, BINS], U8, align_bytes=64)
-            codes_of[units[u]] = (codes, scales)
-            flat = grouped_of[u][:].rearrange("p w j -> p (w j)")
+            codes_of[(n, unit)] = (codes, scales)
+            flat = grouped_of[(n, unit)][:].rearrange("p w j -> p (w j)")
             width = BINS // pieces
             for s in range(pieces):
                 cols = slice(s * width, (s + 1) * width)
@@ -191,11 +200,11 @@ def tile_colourhistogram_t_kernel(tc, image, out):
                     in_=flat[:, s * width * PACK : (s + 1) * width * PACK],
                 )
                 if pieces > 1:
-                    passes(units[u][0], units[u][1], [s])
+                    passes(n, unit[0], [s])
 
         def passes(n, g, blocks):
-            ka, ka_s = codes_of[(n, g, 0)]
-            kb, kb_s = codes_of[(n, g, 1)]
+            ka, ka_s = codes_of[(n, (g, 0))]
+            kb, kb_s = codes_of[(n, (g, 1))]
             for t in blocks:
                 if g == 0:
                     acc = accp.tile([P, BINS], F32)
@@ -211,57 +220,66 @@ def tile_colourhistogram_t_kernel(tc, image, out):
                     stop=(g == PASSES - 1),
                 )
 
-        def drains(n, on_scalar):
-            for t in range(4):
-                res = store.tile([P, BINS], F32)
-                if t < on_scalar:
-                    nc.scalar.copy(out=res[:], in_=acc_of[(n, t)][:])
-                else:
-                    nc.vector.tensor_copy(out=res[:], in_=acc_of[(n, t)][:])
-                nc.sync.dma_start(out=out[n, 0, t * P : (t + 1) * P, :], in_=res[:])
-
-        last = N_IMG - 1
-        for u in range(len(units)):
-            n, g, c = units[u]
-            pos = u % 4
-            if u == FIRST_ARG_STEP:
-                exponent_matmuls(PE_IMAGES[0], range(4))
-            exponentials(u)
-            if pos == 0:
-                product(u)
-                if n >= 1 and units[u - 1] not in codes_of:
-                    quantise(u - 1, 1)
-                    passes(n - 1, 1, range(4))
-            elif pos == 1:
-                product(u)
-                quantise(u - 1, 1)
-            elif pos == 2 and n == last:
-                quantise(u - 1, 1)
-                drains(n - 1, SCALAR_DRAINS[n - 1])
-                passes(n, 0, range(4))
-                product(u)
-            elif pos == 2:
-                product(u)
-                quantise(u - 1, 1)
+        def drain(n, t, on_scalar):
+            res = store.tile([P, BINS], F32)
+            if on_scalar:
+                nc.scalar.copy(out=res[:], in_=acc_of[(n, t)][:])
             else:
-                if from_tensor_engine(u) and n < last:
-                    exponent_matmuls(n + 1, range(ARG_AHEAD))
-                product(u)
-                quantise(u - 1, 1)
+                nc.vector.tensor_copy(out=res[:], in_=acc_of[(n, t)][:])
+            nc.sync.dma_start(out=out[n, 0, t * P : (t + 1) * P, :], in_=res[:])
+
+        exponentials(0, A)
+        exponentials(0, C)
+        for n in range(N_IMG):
+            by_matmul = n in PE_IMAGES
+            exponentials(n, B)
+            if n == last:
+                for t in range(SCALAR_DRAINS[n - 1]):
+                    drain(n - 1, t, True)
+            if by_matmul:
+                exponential_of_bank(n, 0)
+                exponent_matmul(n, 3)
+                exponential_of_bank(n, 1)
                 if n < last:
-                    if n >= 1:
-                        drains(n - 1, SCALAR_DRAINS[n - 1])
-                    passes(n, 0, range(4))
-                if from_tensor_engine(u):
-                    if n == last:
-                        quantise(u, 4)
-                    else:
-                        quantise(u, 1)
-                        passes(n, 1, range(4))
-                        exponent_matmuls(n + 1, range(ARG_AHEAD, 4))
-            if u == 0:
-                later["affine"] = affine(a1, 32 - first, "1")
+                    exponent_matmul(n + 1, 0)
+                exponential_of_bank(n, 2)
+                if n < last:
+                    exponent_matmul(n + 1, 1)
+                    exponentials(n + 1, A)
+                exponential_of_bank(n, 3)
+                if n < last:
+                    exponent_matmul(n + 1, 2)
+                    exponentials(n + 1, C)
+            else:
+                exponentials(n, D)
+                exponentials(n + 1, A)
+                exponentials(n + 1, C)
+            if 1 <= n < last:
+                for t in range(SCALAR_DRAINS[n - 1]):
+                    drain(n - 1, t, True)
+            product(n, A)
+            product_on_gpsimd(n, C)
+            product(n, B)
+            if not by_matmul:
+                product(n, D)
+            if n == 0:
                 spread_and_turn()
-            if u == STATION_STEP:
                 stationary_operands()
-        drains(last, LAST_SCALAR_DRAINS)
+            if n + 1 == PE_IMAGES[0]:
+                for s in range(3):
+                    exponent_matmul(n + 1, s)
+            if n >= 1:
+                for t in range(SCALAR_DRAINS[n - 1], 4):
+                    drain(n - 1, t, False)
+            quantise(n, A, 1)
+            quantise(n, B, 1)
+            passes(n, 0, range(4))
+            if n < last:
+                quantise(n, D, 1)
+                quantise(n, C, 1)
+                passes(n, 1, range(4))
+            else:
+                quantise(n, C, 1)
+                quantise(n, D, 4)
+        for t in range(4):
+            drain(last, t, t < LAST_SCALAR_DRAINS)

@@ -20,7 +20,7 @@ RUN = 4
 KAPPA = 200.0
 FLOPS = 2 * N_IMG * BINS * BINS * 1024
 PE_IMAGES = (2, 3, 4, 5, 6, 7)
-SCALAR_DRAINS = (4, 3, 0, 0, 0, 0, 4)
+SCALAR_DRAINS = (1, 1, 0, 1, 1, 0, 4)
 LAST_SCALAR_DRAINS = 3
 GP_PIECES = 2
 A, B, C, D = (0, 0), (0, 1), (1, 1), (1, 0)
@@ -70,8 +70,6 @@ def tile_colourhistogram_t_kernel(tc, image, out):
             nc.vector.scalar_tensor_tensor(out=bi[:], in0=v[:], scalar=-KAPPA, in1=v[:], op0=ALU.mult, op1=ALU.mult)
             return sc, bi
 
-        sc0, bi0 = affine(a0, first, "0")
-
         head = ident[:, 0 : 3 * PACK]
         term = const.tile([P, 3], F32)
         nc.vector.tensor_reduce(out=term[:], in_=head.rearrange("k (j t) -> k t j", t=3), axis=AX.X, op=ALU.add)
@@ -87,6 +85,7 @@ def tile_colourhistogram_t_kernel(tc, image, out):
         nc.vector.scalar_tensor_tensor(
             out=rows[:], in0=r2[:], scalar=quad[:, 0:1], in1=lin[:], op0=ALU.mult, op1=ALU.add
         )
+        sc0, bi0 = affine(a0, first, "0")
         moving = const.tile([P, BINS, PACK], F32)
         nc.vector.tensor_tensor(
             out=moving[:],
@@ -259,12 +258,12 @@ def tile_colourhistogram_t_kernel(tc, image, out):
                     drain(n - 1, t, True)
             product(n, A)
             product_on_gpsimd(n, C)
-            product(n, B)
-            if not by_matmul:
-                product(n, D)
             if n == 0:
                 spread_and_turn()
                 stationary_operands()
+            product(n, B)
+            if not by_matmul:
+                product(n, D)
             if n + 1 == PE_IMAGES[0]:
                 for s in range(3):
                     exponent_matmul(n + 1, s)

@@ -20,8 +20,8 @@ RUN = 4
 KAPPA = 200.0
 FLOPS = 2 * N_IMG * BINS * BINS * 1024
 PE_IMAGES = (2, 3, 4, 5, 6, 7)
-SCALAR_DRAINS = (1, 1, 0, 1, 1, 0, 4)
-LAST_SCALAR_DRAINS = 3
+SCALAR_DRAINS = (0, 0, 0, 1, 1, 0, 4)
+LAST_SCALAR_DRAINS = 2
 GP_PIECES = 2
 A, B, C, D = (0, 0), (0, 1), (1, 1), (1, 0)
 
@@ -77,6 +77,8 @@ def tile_colourhistogram_t_kernel(tc, image, out):
         nc.vector.tensor_reduce(out=place[:], in_=head.rearrange("k (j t) -> k j t", t=3), axis=AX.X, op=ALU.add)
         quad = const.tile([P, 1], F32)
         nc.vector.tensor_scalar(out=quad[:], in0=term[:, 2:3], scalar1=-KAPPA, scalar2=None, op0=ALU.mult)
+        spread_v = spread[:, :, 0 : 3 * PACK].rearrange("p i (j t) -> p t i j", t=3)
+        nc.vector.memset(spread_v[:, 2], 1.0)
         lin = const.tile([P, BINS], F32)
         nc.vector.tensor_scalar(
             out=lin[:], in0=r[:], scalar1=term[:, 0:1], scalar2=term[:, 1:2], op0=ALU.mult, op1=ALU.add
@@ -101,10 +103,8 @@ def tile_colourhistogram_t_kernel(tc, image, out):
         def spread_and_turn():
             lo = 4 * PE_IMAGES[0] + 1 - first
             hi = 4 * PE_IMAGES[-1] + 1 - first + 1
-            spread_v = spread[:, :, 0 : 3 * PACK].rearrange("p i (j t) -> p t i j", t=3)
-            nc.vector.tensor_copy(out=spread_v[:, 0], in_=sc1[:].rearrange("p (m j) -> p m j", j=PACK)[:, lo:hi:4, :])
-            nc.vector.tensor_copy(out=spread_v[:, 1], in_=bi1[:].rearrange("p (m j) -> p m j", j=PACK)[:, lo:hi:4, :])
-            nc.vector.memset(spread_v[:, 2], 1.0)
+            nc.gpsimd.tensor_copy(out=spread_v[:, 0], in_=sc1[:].rearrange("p (m j) -> p m j", j=PACK)[:, lo:hi:4, :])
+            nc.gpsimd.tensor_copy(out=spread_v[:, 1], in_=bi1[:].rearrange("p (m j) -> p m j", j=PACK)[:, lo:hi:4, :])
             for b in range(0, n_pe, 4):
                 e = min(b + 4, n_pe)
                 turned = argp.tile([P, BINS], F32, tag="arg")
@@ -256,10 +256,11 @@ def tile_colourhistogram_t_kernel(tc, image, out):
             if 1 <= n < last:
                 for t in range(SCALAR_DRAINS[n - 1]):
                     drain(n - 1, t, True)
+            if n == 0:
+                spread_and_turn()
             product(n, A)
             product_on_gpsimd(n, C)
             if n == 0:
-                spread_and_turn()
                 stationary_operands()
             product(n, B)
             if not by_matmul:

@@ -20,9 +20,11 @@ RUN = 4
 KAPPA = 200.0
 FLOPS = 2 * N_IMG * BINS * BINS * 1024
 PE_IMAGES = (2, 3, 4, 5, 6, 7)
-SCALAR_DRAINS = (0, 0, 0, 1, 1, 0, 4)
+SCALAR_DRAINS = (0, 0, 0, 0, 0, 0, 4)
 LAST_SCALAR_DRAINS = 2
 GP_PIECES = 2
+POOL_B = (128, 128, 128, 128, 128, 128, 128, 0)
+POOL_D = (0, 0)
 A, B, C, D = (0, 0), (0, 1), (1, 1), (1, 0)
 
 
@@ -159,18 +161,26 @@ def tile_colourhistogram_t_kernel(tc, image, out):
                 sc, bi = column(m, j)
                 nc.scalar.activation(out=e1[:, j, :], in_=r[:], func=ACT.Exp, bias=bi, scale=sc)
 
-        def product(n, unit):
+        def product(n, unit, bins=BINS):
             grouped = gwork.tile([P, BINS, PACK], BF16, align_bytes=64)
             grouped_of[(n, unit)] = grouped
             nc.vector.tensor_tensor(
-                out=grouped[:].rearrange("p (c i) j -> p c j i", i=RUN),
-                in0=e1_of[(n, unit)][:].rearrange("p j (c i) -> p c j i", i=RUN),
-                in1=gw_psum[:]
+                out=grouped[:, 0:bins, :].rearrange("p (c i) j -> p c j i", i=RUN),
+                in0=e1_of[(n, unit)][:, :, 0:bins].rearrange("p j (c i) -> p c j i", i=RUN),
+                in1=gw_psum[:, 0:bins]
                 .rearrange("p (c i) -> p c i", i=RUN)
                 .unsqueeze(2)
-                .to_broadcast([P, BINS // RUN, PACK, RUN]),
+                .to_broadcast([P, bins // RUN, PACK, RUN]),
                 op=ALU.mult,
             )
+            if bins < BINS:
+                cols = slice(bins, BINS)
+                nc.gpsimd.tensor_tensor(
+                    out=grouped[:, cols, :],
+                    in0=e1_of[(n, unit)][:, :, cols].rearrange("p j w -> p w j"),
+                    in1=gw[:, cols].unsqueeze(2).to_broadcast([P, BINS - bins, PACK]),
+                    op=ALU.mult,
+                )
 
         def product_on_gpsimd(n, unit):
             pgrouped = pwork.tile([P, BINS, PACK], BF16, align_bytes=64)
@@ -262,9 +272,9 @@ def tile_colourhistogram_t_kernel(tc, image, out):
             product_on_gpsimd(n, C)
             if n == 0:
                 stationary_operands()
-            product(n, B)
+            product(n, B, BINS - POOL_B[n])
             if not by_matmul:
-                product(n, D)
+                product(n, D, BINS - POOL_D[n])
             if n + 1 == PE_IMAGES[0]:
                 for s in range(3):
                     exponent_matmul(n + 1, s)
@@ -272,10 +282,11 @@ def tile_colourhistogram_t_kernel(tc, image, out):
                 for t in range(SCALAR_DRAINS[n - 1], 4):
                     drain(n - 1, t, False)
             quantise(n, A, 1)
+            if n < last:
+                quantise(n, D, 1)
             quantise(n, B, 1)
             passes(n, 0, range(4))
             if n < last:
-                quantise(n, D, 1)
                 quantise(n, C, 1)
                 passes(n, 1, range(4))
             else:

@@ -20,10 +20,10 @@ RUN = 4
 KAPPA = 200.0
 FLOPS = 2 * N_IMG * BINS * BINS * 1024
 PE_IMAGES = (2, 3, 4, 5, 6, 7)
-SCALAR_DRAINS = (0, 0, 0, 0, 0, 0, 4)
+SCALAR_DRAINS = (0, 0, 0, 0, 1, 0, 4)
 LAST_SCALAR_DRAINS = 2
-GP_PIECES = 2
-POOL_B = (128, 128, 128, 128, 128, 128, 128, 0)
+GP_PIECES = 1
+POOL_B = (64, 64, 64, 64, 64, 64, 64, 0)
 POOL_D = (0, 0)
 A, B, C, D = (0, 0), (0, 1), (1, 1), (1, 0)
 

@@ -17,10 +17,11 @@ N_IMG = 8
 BINS = 512
 PASSES = 2
 RUN = 4
+HALF = BINS // 2
 KAPPA = 200.0
 FLOPS = 2 * N_IMG * BINS * BINS * 1024
 PE_IMAGES = (2, 3, 4, 5, 6, 7)
-SCALAR_DRAINS = (0, 0, 0, 0, 1, 0, 4)
+SCALAR_DRAINS = (2, 0, 0, 0, 1, 0, 4)
 LAST_SCALAR_DRAINS = 2
 GP_PIECES = 1
 POOL_B = (64, 64, 64, 64, 64, 64, 64, 0)
@@ -55,6 +56,10 @@ def tile_colourhistogram_t_kernel(tc, image, out):
 
         r = const.tile([P, BINS], F32)
         nc.vector.tensor_scalar(out=r[:], in0=idx[:], scalar1=-255.5, scalar2=1.0 / 511.0, op0=ALU.add, op1=ALU.mult)
+        r_split = const.tile([P, BINS], F32)
+        nc.vector.tensor_copy(
+            out=r_split[:].rearrange("p (t m) -> p t m", t=2), in_=r[:].rearrange("p (m t) -> p t m", t=2)
+        )
         r2 = const.tile([P, BINS], F32)
         nc.scalar.activation(out=r2[:], in_=r[:], func=ACT.Square)
         gw = const.tile([P, BINS], F32)
@@ -159,7 +164,39 @@ def tile_colourhistogram_t_kernel(tc, image, out):
             e1_of[(n, unit)] = e1
             for j in range(PACK):
                 sc, bi = column(m, j)
-                nc.scalar.activation(out=e1[:, j, :], in_=r[:], func=ACT.Exp, bias=bi, scale=sc)
+                if n == 0 and unit in (A, D):
+                    nc.scalar.activation(out=e1[:, j, 0:HALF], in_=r_split[:, 0:HALF], func=ACT.Exp, bias=bi, scale=sc)
+                else:
+                    nc.scalar.activation(out=e1[:, j, :], in_=r[:], func=ACT.Exp, bias=bi, scale=sc)
+
+        step = const.tile([P, 2 * PACK], F32)
+
+        def steps():
+            nc.scalar.activation(out=step[:], in_=sc0[:, 0 : 2 * PACK], func=ACT.Exp, scale=1.0 / 511.0)
+
+        def odd_bins(unit):
+            e1 = e1_of[(0, unit)]
+            for j in range(PACK):
+                q = unit[0] * PACK + j
+                nc.vector.tensor_scalar(
+                    out=e1[:, j, HALF:BINS], in0=e1[:, j, 0:HALF], scalar1=step[:, q : q + 1], scalar2=None, op0=ALU.mult
+                )
+
+        def product_split(n, unit):
+            grouped = gwork.tile([P, BINS, PACK], BF16, align_bytes=64)
+            grouped_of[(n, unit)] = grouped
+            for t in range(2):
+                cols = slice(t * HALF, (t + 1) * HALF)
+                nc.vector.tensor_tensor(
+                    out=grouped[:, cols, :].rearrange("p (c i) j -> p c j i", i=RUN),
+                    in0=e1_of[(n, unit)][:, :, cols].rearrange("p j (c i) -> p c j i", i=RUN),
+                    in1=gw_psum[:]
+                    .rearrange("p (m t) -> p t m", t=2)[:, t, :]
+                    .rearrange("p (c i) -> p c i", i=RUN)
+                    .unsqueeze(2)
+                    .to_broadcast([P, HALF // RUN, PACK, RUN]),
+                    op=ALU.mult,
+                )
 
         def product(n, unit, bins=BINS):
             grouped = gwork.tile([P, BINS, PACK], BF16, align_bytes=64)
@@ -235,9 +272,17 @@ def tile_colourhistogram_t_kernel(tc, image, out):
                 nc.scalar.copy(out=res[:], in_=acc_of[(n, t)][:])
             else:
                 nc.vector.tensor_copy(out=res[:], in_=acc_of[(n, t)][:])
-            nc.sync.dma_start(out=out[n, 0, t * P : (t + 1) * P, :], in_=res[:])
+            if n == 0:
+                low = (t % 2) * HALF + t // 2
+                nc.sync.dma_start(out=out[n, 0, low : low + HALF - 1 : 2, :], in_=res[:])
+            else:
+                nc.sync.dma_start(out=out[n, 0, t * P : (t + 1) * P, :], in_=res[:])
 
         exponentials(0, A)
+        steps()
+        odd_bins(A)
+        exponentials(0, D)
+        odd_bins(D)
         exponentials(0, C)
         for n in range(N_IMG):
             by_matmul = n in PE_IMAGES
@@ -260,7 +305,8 @@ def tile_colourhistogram_t_kernel(tc, image, out):
                     exponent_matmul(n + 1, 2)
                     exponentials(n + 1, C)
             else:
-                exponentials(n, D)
+                if n > 0:
+                    exponentials(n, D)
                 exponentials(n + 1, A)
                 exponentials(n + 1, C)
             if 1 <= n < last:
@@ -268,12 +314,15 @@ def tile_colourhistogram_t_kernel(tc, image, out):
                     drain(n - 1, t, True)
             if n == 0:
                 spread_and_turn()
-            product(n, A)
-            product_on_gpsimd(n, C)
             if n == 0:
+                product_split(n, A)
                 stationary_operands()
+                product_split(n, D)
+            else:
+                product(n, A)
+            product_on_gpsimd(n, C)
             product(n, B, BINS - POOL_B[n])
-            if not by_matmul:
+            if n > 0 and not by_matmul:
                 product(n, D, BINS - POOL_D[n])
             if n + 1 == PE_IMAGES[0]:
                 for s in range(3):

@@ -52,7 +52,6 @@ def tile_colourhistogram_t_kernel(tc, image, out):
         ident = const.tile([P, P], F32)
         make_identity(nc, ident[:])
         spread = const.tile([P, n_pe, P], F32)
-        nc.gpsimd.memset(spread[:], 0.0)
 
         r = const.tile([P, BINS], F32)
         nc.vector.tensor_scalar(out=r[:], in0=idx[:], scalar1=-255.5, scalar2=1.0 / 511.0, op0=ALU.add, op1=ALU.mult)
@@ -85,16 +84,17 @@ def tile_colourhistogram_t_kernel(tc, image, out):
         quad = const.tile([P, 1], F32)
         nc.vector.tensor_scalar(out=quad[:], in0=term[:, 2:3], scalar1=-KAPPA, scalar2=None, op0=ALU.mult)
         spread_v = spread[:, :, 0 : 3 * PACK].rearrange("p i (j t) -> p t i j", t=3)
+        nc.vector.memset(spread[:], 0.0)
         nc.vector.memset(spread_v[:, 2], 1.0)
         lin = const.tile([P, BINS], F32)
         nc.vector.tensor_scalar(
             out=lin[:], in0=r[:], scalar1=term[:, 0:1], scalar2=term[:, 1:2], op0=ALU.mult, op1=ALU.add
         )
+        sc0, bi0 = affine(a0, first, "0")
         rows = const.tile([P, BINS], F32)
         nc.vector.scalar_tensor_tensor(
             out=rows[:], in0=r2[:], scalar=quad[:, 0:1], in1=lin[:], op0=ALU.mult, op1=ALU.add
         )
-        sc0, bi0 = affine(a0, first, "0")
         moving = const.tile([P, BINS, PACK], F32)
         nc.vector.tensor_tensor(
             out=moving[:],
@@ -104,10 +104,11 @@ def tile_colourhistogram_t_kernel(tc, image, out):
         )
         moving_flat = moving[:].rearrange("k w j -> k (w j)")
         station = const.tile([P, n_pe, P], F32)
-        sc1, bi1 = affine(a1, 32 - first, "1")
+        late = {}
         turned_of = {}
 
         def spread_and_turn():
+            sc1, bi1 = late["tables"]
             lo = 4 * PE_IMAGES[0] + 1 - first
             hi = 4 * PE_IMAGES[-1] + 1 - first + 1
             nc.gpsimd.tensor_copy(out=spread_v[:, 0], in_=sc1[:].rearrange("p (m j) -> p m j", j=PACK)[:, lo:hi:4, :])
@@ -131,6 +132,7 @@ def tile_colourhistogram_t_kernel(tc, image, out):
                 q = m * PACK + j
                 return sc0[:, q : q + 1], bi0[:, q : q + 1]
             q = (m - first) * PACK + j
+            sc1, bi1 = late["tables"]
             return sc1[:, q : q + 1], bi1[:, q : q + 1]
 
         grouped_of = {}
@@ -283,6 +285,7 @@ def tile_colourhistogram_t_kernel(tc, image, out):
         odd_bins(A)
         exponentials(0, D)
         odd_bins(D)
+        late["tables"] = affine(a1, 32 - first, "1")
         exponentials(0, C)
         for n in range(N_IMG):
             by_matmul = n in PE_IMAGES

@@ -22,7 +22,6 @@ KAPPA = 200.0
 FLOPS = 2 * N_IMG * BINS * BINS * 1024
 PE_IMAGES = (2, 3, 4, 5, 6, 7)
 SCALAR_DRAINS = (2, 0, 0, 0, 1, 0, 4)
-LAST_SCALAR_DRAINS = 2
 GP_PIECES = 1
 POOL_B = (64, 64, 64, 64, 64, 64, 64, 0)
 POOL_D = (0, 0)
@@ -53,6 +52,9 @@ def tile_colourhistogram_t_kernel(tc, image, out):
         make_identity(nc, ident[:])
         spread = const.tile([P, n_pe, P], F32)
 
+        spread_v = spread[:, :, 0 : 3 * PACK].rearrange("p i (j t) -> p t i j", t=3)
+        nc.vector.memset(spread[:], 0.0)
+        nc.vector.memset(spread_v[:, 2], 1.0)
         r = const.tile([P, BINS], F32)
         nc.vector.tensor_scalar(out=r[:], in0=idx[:], scalar1=-255.5, scalar2=1.0 / 511.0, op0=ALU.add, op1=ALU.mult)
         r_split = const.tile([P, BINS], F32)
@@ -83,9 +85,6 @@ def tile_colourhistogram_t_kernel(tc, image, out):
         nc.vector.tensor_reduce(out=place[:], in_=head.rearrange("k (j t) -> k j t", t=3), axis=AX.X, op=ALU.add)
         quad = const.tile([P, 1], F32)
         nc.vector.tensor_scalar(out=quad[:], in0=term[:, 2:3], scalar1=-KAPPA, scalar2=None, op0=ALU.mult)
-        spread_v = spread[:, :, 0 : 3 * PACK].rearrange("p i (j t) -> p t i j", t=3)
-        nc.vector.memset(spread[:], 0.0)
-        nc.vector.memset(spread_v[:, 2], 1.0)
         lin = const.tile([P, BINS], F32)
         nc.vector.tensor_scalar(
             out=lin[:], in0=r[:], scalar1=term[:, 0:1], scalar2=term[:, 1:2], op0=ALU.mult, op1=ALU.add
@@ -95,14 +94,22 @@ def tile_colourhistogram_t_kernel(tc, image, out):
         nc.vector.scalar_tensor_tensor(
             out=rows[:], in0=r2[:], scalar=quad[:, 0:1], in1=lin[:], op0=ALU.mult, op1=ALU.add
         )
-        moving = const.tile([P, BINS, PACK], F32)
-        nc.vector.tensor_tensor(
-            out=moving[:],
-            in0=rows[:].unsqueeze(2).to_broadcast([P, BINS, PACK]),
-            in1=place[:].unsqueeze(1).to_broadcast([P, BINS, PACK]),
-            op=ALU.mult,
-        )
-        moving_flat = moving[:].rearrange("k w j -> k (w j)")
+        moving = const.tile([P, PACK, PACK, P], F32)
+
+        def moving_slot(j):
+            nc.vector.tensor_scalar(
+                out=moving[:, :, j, :],
+                in0=rows[:].rearrange("k (s w) -> k s w", w=P),
+                scalar1=place[:, j : j + 1],
+                scalar2=None,
+                op0=ALU.mult,
+            )
+
+
+        moving_slot(0)
+        moving_slot(1)
+        moving_slot(2)
+        moving_slot(3)
         station = const.tile([P, n_pe, P], F32)
         late = {}
         turned_of = {}
@@ -147,7 +154,7 @@ def tile_colourhistogram_t_kernel(tc, image, out):
             nc.tensor.matmul(
                 out=arg[:],
                 lhsT=station[:, PE_IMAGES.index(n), :],
-                rhs=moving_flat[:, s * BINS : (s + 1) * BINS],
+                rhs=moving[:, s, :, :].rearrange("k j w -> k (j w)"),
                 start=True,
                 stop=True,
             )
@@ -156,8 +163,11 @@ def tile_colourhistogram_t_kernel(tc, image, out):
             if s == 0:
                 grouped = gwork.tile([P, BINS, PACK], BF16, align_bytes=64)
                 grouped_of[(n, D)] = grouped
-            flat = grouped_of[(n, D)][:].rearrange("p w j -> p (w j)")
-            nc.scalar.activation(out=flat[:, s * BINS : (s + 1) * BINS], in_=arg_of[(n, s)][:], func=ACT.Exp)
+            nc.scalar.activation(
+                out=grouped_of[(n, D)][:, s * P : (s + 1) * P, :],
+                in_=arg_of[(n, s)][:].rearrange("p (j w) -> p w j", j=PACK),
+                func=ACT.Exp,
+            )
 
         def exponentials(n, unit):
             g, c = unit
@@ -345,4 +355,4 @@ def tile_colourhistogram_t_kernel(tc, image, out):
                 quantise(n, C, 1)
                 quantise(n, D, 4)
         for t in range(4):
-            drain(last, t, t < LAST_SCALAR_DRAINS)
+            drain(last, t, t % 2 == 0)

@@ -21,10 +21,11 @@ HALF = BINS // 2
 KAPPA = 200.0
 FLOPS = 2 * N_IMG * BINS * BINS * 1024
 PE_IMAGES = (2, 3, 4, 5, 6, 7)
-SCALAR_DRAINS = (2, 0, 0, 0, 1, 0, 4)
-GP_PIECES = 1
-POOL_B = (64, 64, 64, 64, 64, 64, 64, 0)
-POOL_D = (0, 0)
+SHIFT = 16
+SHIFTED_FROM = 2
+SHIFTED_SLOTS = 1
+SCALAR_DRAINS = (4, 0, 0, 1, 1, 1, 4)
+LAST_SHARED_BINS = 64
 A, B, C, D = (0, 0), (0, 1), (1, 1), (1, 0)
 
 
@@ -90,6 +91,7 @@ def tile_colourhistogram_t_kernel(tc, image, out):
             out=lin[:], in0=r[:], scalar1=term[:, 0:1], scalar2=term[:, 1:2], op0=ALU.mult, op1=ALU.add
         )
         sc0, bi0 = affine(a0, first, "0")
+        st1 = const.tile([P, (32 - first) * PACK], F32)
         rows = const.tile([P, BINS], F32)
         nc.vector.scalar_tensor_tensor(
             out=rows[:], in0=r2[:], scalar=quad[:, 0:1], in1=lin[:], op0=ALU.mult, op1=ALU.add
@@ -105,11 +107,8 @@ def tile_colourhistogram_t_kernel(tc, image, out):
                 op0=ALU.mult,
             )
 
-
-        moving_slot(0)
-        moving_slot(1)
-        moving_slot(2)
-        moving_slot(3)
+        for j in range(PACK):
+            moving_slot(j)
         station = const.tile([P, n_pe, P], F32)
         late = {}
         turned_of = {}
@@ -176,10 +175,51 @@ def tile_colourhistogram_t_kernel(tc, image, out):
             e1_of[(n, unit)] = e1
             for j in range(PACK):
                 sc, bi = column(m, j)
-                if n == 0 and unit in (A, D):
+                if n == 0 and unit == C:
+                    nc.scalar.activation(out=halves(e1[:, j, :], 0), in_=halves(r[:], 0), func=ACT.Exp, bias=bi, scale=sc)
+                elif n == 0 and unit in (A, D):
                     nc.scalar.activation(out=e1[:, j, 0:HALF], in_=r_split[:, 0:HALF], func=ACT.Exp, bias=bi, scale=sc)
+                elif n >= SHIFTED_FROM and unit == A and j < SHIFTED_SLOTS:
+                    nc.scalar.activation(out=halves(e1[:, j, :], 0), in_=halves(r[:], 0), func=ACT.Exp, bias=bi, scale=sc)
                 else:
                     nc.scalar.activation(out=e1[:, j, :], in_=r[:], func=ACT.Exp, bias=bi, scale=sc)
+
+        def shift_steps():
+            nc.scalar.activation(out=st1[:], in_=late["tables"][0][:], func=ACT.Exp, scale=SHIFT / 511.0)
+
+        def shifted(n):
+            if n < SHIFTED_FROM:
+                return
+            m = n * 2 * PASSES
+            e1 = e1_of[(n, A)]
+            for j in range(SHIFTED_SLOTS):
+                q = (m - first) * PACK + j
+                nc.gpsimd.tensor_scalar(
+                    out=halves(e1[:, j, :], 1),
+                    in0=halves(e1[:, j, :], 0),
+                    scalar1=st1[:, q : q + 1],
+                    scalar2=0.0,
+                    op0=ALU.mult,
+                    op1=ALU.add,
+                )
+
+        def halves(x, h):
+            return x.rearrange("p (c h i) -> p c h i", h=2, i=SHIFT)[:, :, h, :]
+
+        leap = const.tile([P, PACK], F32)
+
+        def upper_halves():
+            e1 = e1_of[(0, C)]
+            nc.scalar.activation(out=leap[:], in_=sc0[:, 3 * PACK : 4 * PACK], func=ACT.Exp, scale=SHIFT / 511.0)
+            for j in range(PACK):
+                nc.gpsimd.tensor_scalar(
+                    out=halves(e1[:, j, :], 1),
+                    in0=halves(e1[:, j, :], 0),
+                    scalar1=leap[:, j : j + 1],
+                    scalar2=0.0,
+                    op0=ALU.mult,
+                    op1=ALU.add,
+                )
 
         step = const.tile([P, 2 * PACK], F32)
 
@@ -191,7 +231,12 @@ def tile_colourhistogram_t_kernel(tc, image, out):
             for j in range(PACK):
                 q = unit[0] * PACK + j
                 nc.vector.tensor_scalar(
-                    out=e1[:, j, HALF:BINS], in0=e1[:, j, 0:HALF], scalar1=step[:, q : q + 1], scalar2=None, op0=ALU.mult
+                    out=e1[:, j, HALF:BINS],
+                    in0=e1[:, j, 0:HALF],
+                    scalar1=step[:, q : q + 1],
+                    scalar2=0.0,
+                    op0=ALU.mult,
+                    op1=ALU.add,
                 )
 
         def product_split(n, unit):
@@ -210,37 +255,37 @@ def tile_colourhistogram_t_kernel(tc, image, out):
                     op=ALU.mult,
                 )
 
-        def product(n, unit, bins=BINS):
+        def product(n, unit):
             grouped = gwork.tile([P, BINS, PACK], BF16, align_bytes=64)
             grouped_of[(n, unit)] = grouped
             nc.vector.tensor_tensor(
-                out=grouped[:, 0:bins, :].rearrange("p (c i) j -> p c j i", i=RUN),
-                in0=e1_of[(n, unit)][:, :, 0:bins].rearrange("p j (c i) -> p c j i", i=RUN),
-                in1=gw_psum[:, 0:bins]
+                out=grouped[:].rearrange("p (c i) j -> p c j i", i=RUN),
+                in0=e1_of[(n, unit)][:].rearrange("p j (c i) -> p c j i", i=RUN),
+                in1=gw_psum[:]
                 .rearrange("p (c i) -> p c i", i=RUN)
                 .unsqueeze(2)
-                .to_broadcast([P, bins // RUN, PACK, RUN]),
+                .to_broadcast([P, BINS // RUN, PACK, RUN]),
                 op=ALU.mult,
             )
-            if bins < BINS:
-                cols = slice(bins, BINS)
-                nc.gpsimd.tensor_tensor(
-                    out=grouped[:, cols, :],
-                    in0=e1_of[(n, unit)][:, :, cols].rearrange("p j w -> p w j"),
-                    in1=gw[:, cols].unsqueeze(2).to_broadcast([P, BINS - bins, PACK]),
-                    op=ALU.mult,
-                )
 
         def product_on_gpsimd(n, unit):
             pgrouped = pwork.tile([P, BINS, PACK], BF16, align_bytes=64)
             grouped_of[(n, unit)] = pgrouped
-            width = BINS // GP_PIECES
-            for h in range(GP_PIECES):
-                cols = slice(h * width, (h + 1) * width)
-                nc.gpsimd.tensor_tensor(
-                    out=pgrouped[:, cols, :],
-                    in0=e1_of[(n, unit)][:, :, cols].rearrange("p j w -> p w j"),
-                    in1=gw[:, cols].unsqueeze(2).to_broadcast([P, width, PACK]),
+            width = BINS - LAST_SHARED_BINS if n == last else BINS
+            nc.gpsimd.tensor_tensor(
+                out=pgrouped[:, 0:width, :],
+                in0=e1_of[(n, unit)][:, :, 0:width].rearrange("p j w -> p w j"),
+                in1=gw[:, 0:width].unsqueeze(2).to_broadcast([P, width, PACK]),
+                op=ALU.mult,
+            )
+            if width < BINS:
+                nc.vector.tensor_tensor(
+                    out=pgrouped[:, width:BINS, :].rearrange("p (c i) j -> p c j i", i=RUN),
+                    in0=e1_of[(n, unit)][:, :, width:BINS].rearrange("p j (c i) -> p c j i", i=RUN),
+                    in1=gw_psum[:, width:BINS]
+                    .rearrange("p (c i) -> p c i", i=RUN)
+                    .unsqueeze(2)
+                    .to_broadcast([P, (BINS - width) // RUN, PACK, RUN]),
                     op=ALU.mult,
                 )
 
@@ -297,12 +342,13 @@ def tile_colourhistogram_t_kernel(tc, image, out):
         odd_bins(D)
         late["tables"] = affine(a1, 32 - first, "1")
         exponentials(0, C)
+        spread_and_turn()
+        upper_halves()
         for n in range(N_IMG):
             by_matmul = n in PE_IMAGES
             exponentials(n, B)
-            if n == last:
-                for t in range(SCALAR_DRAINS[n - 1]):
-                    drain(n - 1, t, True)
+            if n == 0:
+                shift_steps()
             if by_matmul:
                 exponential_of_bank(n, 0)
                 exponent_matmul(n, 3)
@@ -313,6 +359,9 @@ def tile_colourhistogram_t_kernel(tc, image, out):
                 if n < last:
                     exponent_matmul(n + 1, 1)
                     exponentials(n + 1, A)
+                if n == last:
+                    for t in range(SCALAR_DRAINS[n - 1]):
+                        drain(n - 1, t, True)
                 exponential_of_bank(n, 3)
                 if n < last:
                     exponent_matmul(n + 1, 2)
@@ -326,17 +375,17 @@ def tile_colourhistogram_t_kernel(tc, image, out):
                 for t in range(SCALAR_DRAINS[n - 1]):
                     drain(n - 1, t, True)
             if n == 0:
-                spread_and_turn()
-            if n == 0:
                 product_split(n, A)
-                stationary_operands()
                 product_split(n, D)
+                stationary_operands()
             else:
                 product(n, A)
             product_on_gpsimd(n, C)
-            product(n, B, BINS - POOL_B[n])
+            if n < last:
+                shifted(n + 1)
+            product(n, B)
             if n > 0 and not by_matmul:
-                product(n, D, BINS - POOL_D[n])
+                product(n, D)
             if n + 1 == PE_IMAGES[0]:
                 for s in range(3):
                     exponent_matmul(n + 1, s)

@@ -303,7 +303,9 @@ def tile_colourhistogram_t_kernel(tc, image, out):
                     in_=flat[:, s * width * PACK : (s + 1) * width * PACK],
                 )
                 if pieces > 1:
-                    passes(n, unit[0], [s])
+                    passes(n, 1, [s])
+                    if s + 2 < pieces:
+                        passes(n, 0, [s + 2])
 
         def passes(n, g, blocks):
             ka, ka_s = codes_of[(n, (g, 0))]
@@ -396,7 +398,7 @@ def tile_colourhistogram_t_kernel(tc, image, out):
             if n < last:
                 quantise(n, D, 1)
             quantise(n, B, 1)
-            passes(n, 0, range(4))
+            passes(n, 0, range(4 if n < last else 2))
             if n < last:
                 quantise(n, C, 1)
                 passes(n, 1, range(4))

import concourse.mybir as mybir
from concourse.masks import make_identity

F32 = mybir.dt.float32
BF16 = mybir.dt.bfloat16
I32 = mybir.dt.int32
U32 = mybir.dt.uint32
U8 = mybir.dt.uint8
FP8X4 = mybir.dt.float8_e4m3fn_x4
ACT = mybir.ActivationFunctionType
ALU = mybir.AluOpType
AX = mybir.AxisListType

P = 128
PACK = 4
N_IMG = 8
BINS = 512
PASSES = 2
RUN = 4
HALF = BINS // 2
KAPPA = 200.0
FLOPS = 2 * N_IMG * BINS * BINS * 1024
PE_IMAGES = (2, 3, 4, 5, 6, 7)
SHIFT = 16
SHIFTED_FROM = 2
SHIFTED_SLOTS = 1
SCALAR_DRAINS = (4, 0, 0, 1, 1, 1, 4)
LAST_SHARED_BINS = 64
A, B, C, D = (0, 0), (0, 1), (1, 1), (1, 0)


def tile_colourhistogram_t_kernel(tc, image, out):
    nc = tc.nc
    pix = image.rearrange("n c (g hp) (wp j) -> (hp wp) (n c g) j", g=PASSES, hp=16, wp=8, j=PACK)
    n_pe = len(PE_IMAGES)
    last = N_IMG - 1
    with tc.tile_pool(name="const", bufs=1) as const, tc.tile_pool(name="ework", bufs=6) as ework, tc.tile_pool(
        name="gwork", bufs=6
    ) as gwork, tc.tile_pool(name="pwork", bufs=1) as pwork, tc.tile_pool(name="quant", bufs=8) as quant, tc.tile_pool(
        name="store", bufs=6
    ) as store, tc.psum_pool(name="accp", bufs=4) as accp, tc.psum_pool(name="argp", bufs=3) as argp, tc.psum_pool(
        name="gpsum", bufs=1
    ) as gpsum, tc.manual_schedule():
        first = 4
        a0 = const.tile([P, first, PACK], BF16)
        a1 = const.tile([P, 32 - first, PACK], BF16)
        nc.sync.dma_start(out=a0[:], in_=pix[:, 0:first, :])
        nc.sync.dma_start(out=a1[:], in_=pix[:, first:32, :])

        idx = const.tile([P, BINS], I32)
        nc.gpsimd.iota(idx[:], pattern=[[1, BINS]], base=0, channel_multiplier=0)
        ident = const.tile([P, P], F32)
        make_identity(nc, ident[:])
        spread = const.tile([P, n_pe, P], F32)

        spread_v = spread[:, :, 0 : 3 * PACK].rearrange("p i (j t) -> p t i j", t=3)
        nc.vector.memset(spread[:], 0.0)
        nc.vector.memset(spread_v[:, 2], 1.0)
        r = const.tile([P, BINS], F32)
        nc.vector.tensor_scalar(out=r[:], in0=idx[:], scalar1=-255.5, scalar2=1.0 / 511.0, op0=ALU.add, op1=ALU.mult)
        r_split = const.tile([P, BINS], F32)
        nc.vector.tensor_copy(
            out=r_split[:].rearrange("p (t m) -> p t m", t=2), in_=r[:].rearrange("p (m t) -> p t m", t=2)
        )
        r2 = const.tile([P, BINS], F32)
        nc.scalar.activation(out=r2[:], in_=r[:], func=ACT.Square)
        gw = const.tile([P, BINS], F32)
        nc.scalar.activation(out=gw[:], in_=r2[:], func=ACT.Exp, scale=-KAPPA)
        gw_psum = gpsum.tile([P, BINS], F32)
        nc.tensor.matmul(out=gw_psum[:], lhsT=ident[:], rhs=gw[:], start=True, stop=True)

        def affine(a, cols, label):
            v = const.tile([P, cols * PACK], F32, name="v" + label)
            sc = const.tile([P, cols * PACK], F32, name="sc" + label)
            bi = const.tile([P, cols * PACK], F32, name="bi" + label)
            flat = a[:].rearrange("p m j -> p (m j)")
            nc.vector.tensor_scalar(out=v[:], in0=flat, scalar1=-0.5, scalar2=None, op0=ALU.add)
            nc.vector.tensor_scalar(out=sc[:], in0=flat, scalar1=-0.5, scalar2=2.0 * KAPPA, op0=ALU.add, op1=ALU.mult)
            nc.vector.scalar_tensor_tensor(out=bi[:], in0=v[:], scalar=-KAPPA, in1=v[:], op0=ALU.mult, op1=ALU.mult)
            return sc, bi

        head = ident[:, 0 : 3 * PACK]
        term = const.tile([P, 3], F32)
        nc.vector.tensor_reduce(out=term[:], in_=head.rearrange("k (j t) -> k t j", t=3), axis=AX.X, op=ALU.add)
        place = const.tile([P, PACK], F32)
        nc.vector.tensor_reduce(out=place[:], in_=head.rearrange("k (j t) -> k j t", t=3), axis=AX.X, op=ALU.add)
        quad = const.tile([P, 1], F32)
        nc.vector.tensor_scalar(out=quad[:], in0=term[:, 2:3], scalar1=-KAPPA, scalar2=None, op0=ALU.mult)
        lin = const.tile([P, BINS], F32)
        nc.vector.tensor_scalar(
            out=lin[:], in0=r[:], scalar1=term[:, 0:1], scalar2=term[:, 1:2], op0=ALU.mult, op1=ALU.add
        )
        sc0, bi0 = affine(a0, first, "0")
        st1 = const.tile([P, (32 - first) * PACK], F32)
        rows = const.tile([P, BINS], F32)
        nc.vector.scalar_tensor_tensor(
            out=rows[:], in0=r2[:], scalar=quad[:, 0:1], in1=lin[:], op0=ALU.mult, op1=ALU.add
        )
        moving = const.tile([P, PACK, PACK, P], F32)

        def moving_slot(j):
            nc.vector.tensor_scalar(
                out=moving[:, :, j, :],
                in0=rows[:].rearrange("k (s w) -> k s w", w=P),
                scalar1=place[:, j : j + 1],
                scalar2=None,
                op0=ALU.mult,
            )

        for j in range(PACK):
            moving_slot(j)
        station = const.tile([P, n_pe, P], F32)
        late = {}
        turned_of = {}

        def spread_and_turn():
            sc1, bi1 = late["tables"]
            lo = 4 * PE_IMAGES[0] + 1 - first
            hi = 4 * PE_IMAGES[-1] + 1 - first + 1
            nc.gpsimd.tensor_copy(out=spread_v[:, 0], in_=sc1[:].rearrange("p (m j) -> p m j", j=PACK)[:, lo:hi:4, :])
            nc.gpsimd.tensor_copy(out=spread_v[:, 1], in_=bi1[:].rearrange("p (m j) -> p m j", j=PACK)[:, lo:hi:4, :])
            for b in range(0, n_pe, 4):
                e = min(b + 4, n_pe)
                turned = argp.tile([P, BINS], F32, tag="arg")
                turned_of[b] = turned
                for i in range(b, e):
                    nc.tensor.transpose(turned[:, (i - b) * P : (i - b + 1) * P], spread[:, i, :], ident[:])

        def stationary_operands():
            for b in range(0, n_pe, 4):
                e = min(b + 4, n_pe)
                nc.vector.tensor_copy(
                    out=station[:, b:e, :].rearrange("k i p -> k (i p)"), in_=turned_of[b][:, 0 : (e - b) * P]
                )

        def column(m, j):
            if m < first:
                q = m * PACK + j
                return sc0[:, q : q + 1], bi0[:, q : q + 1]
            q = (m - first) * PACK + j
            sc1, bi1 = late["tables"]
            return sc1[:, q : q + 1], bi1[:, q : q + 1]

        grouped_of = {}
        codes_of = {}
        acc_of = {}
        arg_of = {}
        e1_of = {}

        def exponent_matmul(n, s):
            arg = argp.tile([P, BINS], F32, tag="arg")
            arg_of[(n, s)] = arg
            nc.tensor.matmul(
                out=arg[:],
                lhsT=station[:, PE_IMAGES.index(n), :],
                rhs=moving[:, s, :, :].rearrange("k j w -> k (j w)"),
                start=True,
                stop=True,
            )

        def exponential_of_bank(n, s):
            if s == 0:
                grouped = gwork.tile([P, BINS, PACK], BF16, align_bytes=64)
                grouped_of[(n, D)] = grouped
            nc.scalar.activation(
                out=grouped_of[(n, D)][:, s * P : (s + 1) * P, :],
                in_=arg_of[(n, s)][:].rearrange("p (j w) -> p w j", j=PACK),
                func=ACT.Exp,
            )

        def exponentials(n, unit):
            g, c = unit
            m = (n * 2 + c) * PASSES + g
            e1 = ework.tile([P, PACK, BINS], F32)
            e1_of[(n, unit)] = e1
            for j in range(PACK):
                sc, bi = column(m, j)
                if n == 0 and unit == C:
                    nc.scalar.activation(out=halves(e1[:, j, :], 0), in_=halves(r[:], 0), func=ACT.Exp, bias=bi, scale=sc)
                elif n == 0 and unit in (A, D):
                    nc.scalar.activation(out=e1[:, j, 0:HALF], in_=r_split[:, 0:HALF], func=ACT.Exp, bias=bi, scale=sc)
                elif n >= SHIFTED_FROM and unit == A and j < SHIFTED_SLOTS:
                    nc.scalar.activation(out=halves(e1[:, j, :], 0), in_=halves(r[:], 0), func=ACT.Exp, bias=bi, scale=sc)
                else:
                    nc.scalar.activation(out=e1[:, j, :], in_=r[:], func=ACT.Exp, bias=bi, scale=sc)

        def shift_steps():
            nc.scalar.activation(out=st1[:], in_=late["tables"][0][:], func=ACT.Exp, scale=SHIFT / 511.0)

        def shifted(n):
            if n < SHIFTED_FROM:
                return
            m = n * 2 * PASSES
            e1 = e1_of[(n, A)]
            for j in range(SHIFTED_SLOTS):
                q = (m - first) * PACK + j
                nc.gpsimd.tensor_scalar(
                    out=halves(e1[:, j, :], 1),
                    in0=halves(e1[:, j, :], 0),
                    scalar1=st1[:, q : q + 1],
                    scalar2=0.0,
                    op0=ALU.mult,
                    op1=ALU.add,
                )

        def halves(x, h):
            return x.rearrange("p (c h i) -> p c h i", h=2, i=SHIFT)[:, :, h, :]

        leap = const.tile([P, PACK], F32)

        def upper_halves():
            e1 = e1_of[(0, C)]
            nc.scalar.activation(out=leap[:], in_=sc0[:, 3 * PACK : 4 * PACK], func=ACT.Exp, scale=SHIFT / 511.0)
            for j in range(PACK):
                nc.gpsimd.tensor_scalar(
                    out=halves(e1[:, j, :], 1),
                    in0=halves(e1[:, j, :], 0),
                    scalar1=leap[:, j : j + 1],
                    scalar2=0.0,
                    op0=ALU.mult,
                    op1=ALU.add,
                )

        step = const.tile([P, 2 * PACK], F32)

        def steps():
            nc.scalar.activation(out=step[:], in_=sc0[:, 0 : 2 * PACK], func=ACT.Exp, scale=1.0 / 511.0)

        def odd_bins(unit):
            e1 = e1_of[(0, unit)]
            for j in range(PACK):
                q = unit[0] * PACK + j
                nc.vector.tensor_scalar(
                    out=e1[:, j, HALF:BINS],
                    in0=e1[:, j, 0:HALF],
                    scalar1=step[:, q : q + 1],
                    scalar2=0.0,
                    op0=ALU.mult,
                    op1=ALU.add,
                )

        def product_split(n, unit):
            grouped = gwork.tile([P, BINS, PACK], BF16, align_bytes=64)
            grouped_of[(n, unit)] = grouped
            for t in range(2):
                cols = slice(t * HALF, (t + 1) * HALF)
                nc.vector.tensor_tensor(
                    out=grouped[:, cols, :].rearrange("p (c i) j -> p c j i", i=RUN),
                    in0=e1_of[(n, unit)][:, :, cols].rearrange("p j (c i) -> p c j i", i=RUN),
                    in1=gw_psum[:]
                    .rearrange("p (m t) -> p t m", t=2)[:, t, :]
                    .rearrange("p (c i) -> p c i", i=RUN)
                    .unsqueeze(2)
                    .to_broadcast([P, HALF // RUN, PACK, RUN]),
                    op=ALU.mult,
                )

        def product(n, unit):
            grouped = gwork.tile([P, BINS, PACK], BF16, align_bytes=64)
            grouped_of[(n, unit)] = grouped
            nc.vector.tensor_tensor(
                out=grouped[:].rearrange("p (c i) j -> p c j i", i=RUN),
                in0=e1_of[(n, unit)][:].rearrange("p j (c i) -> p c j i", i=RUN),
                in1=gw_psum[:]
                .rearrange("p (c i) -> p c i", i=RUN)
                .unsqueeze(2)
                .to_broadcast([P, BINS // RUN, PACK, RUN]),
                op=ALU.mult,
            )

        def product_on_gpsimd(n, unit):
            pgrouped = pwork.tile([P, BINS, PACK], BF16, align_bytes=64)
            grouped_of[(n, unit)] = pgrouped
            width = BINS - LAST_SHARED_BINS if n == last else BINS
            nc.gpsimd.tensor_tensor(
                out=pgrouped[:, 0:width, :],
                in0=e1_of[(n, unit)][:, :, 0:width].rearrange("p j w -> p w j"),
                in1=gw[:, 0:width].unsqueeze(2).to_broadcast([P, width, PACK]),
                op=ALU.mult,
            )
            if width < BINS:
                nc.vector.tensor_tensor(
                    out=pgrouped[:, width:BINS, :].rearrange("p (c i) j -> p c j i", i=RUN),
                    in0=e1_of[(n, unit)][:, :, width:BINS].rearrange("p j (c i) -> p c j i", i=RUN),
                    in1=gw_psum[:, width:BINS]
                    .rearrange("p (c i) -> p c i", i=RUN)
                    .unsqueeze(2)
                    .to_broadcast([P, (BINS - width) // RUN, PACK, RUN]),
                    op=ALU.mult,
                )

        def quantise(n, unit, pieces):
            codes = quant.tile([P, BINS], U32, align_bytes=64)
            scales = quant.tile([P, BINS], U8, align_bytes=64)
            codes_of[(n, unit)] = (codes, scales)
            flat = grouped_of[(n, unit)][:].rearrange("p w j -> p (w j)")
            width = BINS // pieces
            for s in range(pieces):
                cols = slice(s * width, (s + 1) * width)
                nc.vector.quantize_mx(
                    out=codes[:, cols].bitcast(FP8X4),
                    scales=scales[:, cols],
                    in_=flat[:, s * width * PACK : (s + 1) * width * PACK],
                )
                if pieces > 1:
                    passes(n, 1, [s])
                    if s + 2 < pieces:
                        passes(n, 0, [s + 2])

        def passes(n, g, blocks):
            ka, ka_s = codes_of[(n, (g, 0))]
            kb, kb_s = codes_of[(n, (g, 1))]
            for t in blocks:
                if g == 0:
                    acc = accp.tile([P, BINS], F32)
                    acc_of[(n, t)] = acc
                cols = slice(t * P, (t + 1) * P)
                nc.tensor.matmul_mx(
                    out=acc_of[(n, t)][:],
                    lhsT=ka[:, cols].bitcast(FP8X4),
                    lhsT_scale=ka_s[:, cols],
                    rhs=kb[:].bitcast(FP8X4),
                    rhs_scale=kb_s[:],
                    start=(g == 0),
                    stop=(g == PASSES - 1),
                )

        def drain(n, t, on_scalar):
            res = store.tile([P, BINS], F32)
            if on_scalar:
                nc.scalar.copy(out=res[:], in_=acc_of[(n, t)][:])
            else:
                nc.vector.tensor_copy(out=res[:], in_=acc_of[(n, t)][:])
            if n == 0:
                low = (t % 2) * HALF + t // 2
                nc.sync.dma_start(out=out[n, 0, low : low + HALF - 1 : 2, :], in_=res[:])
            else:
                nc.sync.dma_start(out=out[n, 0, t * P : (t + 1) * P, :], in_=res[:])

        exponentials(0, A)
        steps()
        odd_bins(A)
        exponentials(0, D)
        odd_bins(D)
        late["tables"] = affine(a1, 32 - first, "1")
        exponentials(0, C)
        spread_and_turn()
        upper_halves()
        for n in range(N_IMG):
            by_matmul = n in PE_IMAGES
            exponentials(n, B)
            if n == 0:
                shift_steps()
            if by_matmul:
                exponential_of_bank(n, 0)
                exponent_matmul(n, 3)
                exponential_of_bank(n, 1)
                if n < last:
                    exponent_matmul(n + 1, 0)
                exponential_of_bank(n, 2)
                if n < last:
                    exponent_matmul(n + 1, 1)
                    exponentials(n + 1, A)
                if n == last:
                    for t in range(SCALAR_DRAINS[n - 1]):
                        drain(n - 1, t, True)
                exponential_of_bank(n, 3)
                if n < last:
                    exponent_matmul(n + 1, 2)
                    exponentials(n + 1, C)
            else:
                if n > 0:
                    exponentials(n, D)
                exponentials(n + 1, A)
                exponentials(n + 1, C)
            if 1 <= n < last:
                for t in range(SCALAR_DRAINS[n - 1]):
                    drain(n - 1, t, True)
            if n == 0:
                product_split(n, A)
                product_split(n, D)
                stationary_operands()
            else:
                product(n, A)
            product_on_gpsimd(n, C)
            if n < last:
                shifted(n + 1)
            product(n, B)
            if n > 0 and not by_matmul:
                product(n, D)
            if n + 1 == PE_IMAGES[0]:
                for s in range(3):
                    exponent_matmul(n + 1, s)
            if n >= 1:
                for t in range(SCALAR_DRAINS[n - 1], 4):
                    drain(n - 1, t, False)
            quantise(n, A, 1)
            if n < last:
                quantise(n, D, 1)
            quantise(n, B, 1)
            passes(n, 0, range(4 if n < last else 2))
            if n < last:
                quantise(n, C, 1)
                passes(n, 1, range(4))
            else:
                quantise(n, C, 1)
                quantise(n, D, 4)
        for t in range(4):
            drain(last, t, t % 2 == 0)
